import numpy as np
import ml_dtypes


def mxq(x, axis, fmt="e4m3"):
    dtype, down = {"e4m3": (ml_dtypes.float8_e4m3fn, 7), "e5m2": (ml_dtypes.float8_e5m2, 14)}[fmt]
    v = np.moveaxis(np.asarray(x, np.float32).astype(ml_dtypes.bfloat16).astype(np.float64), axis, -1)
    blocks = v.reshape(v.shape[:-1] + (-1, 32))
    amax = np.abs(blocks).max(-1, keepdims=True)
    byte = np.maximum(np.where(amax > 0, np.frexp(amax)[1] - 1 + 127, 0) - down, 1)
    scale = np.exp2(byte - 127.0)
    codes = (blocks / scale).astype(np.float32).astype(dtype).astype(np.float64)
    return np.moveaxis((codes * scale).reshape(v.shape), -1, axis)


WIDE = False


def mx_kscale(k):
    if not WIDE:
        return np.ones(k)
    levels = np.array([10, -10, 5, -5, 0])
    a = np.random.permutation(np.resize(levels, k // 512 * 4)).reshape(k // 512, 4)
    idx = np.arange(k)
    return np.exp2(a[idx // 512, idx % 128 // 32])


BF16 = ml_dtypes.bfloat16


def bf(x):
    return np.asarray(x, np.float32).astype(BF16)


def f64(x):
    return np.asarray(x).astype(np.float64)


B, HALF, MID = 8192, 128, 512
D = 2 * HALF


def setup_inputs():
    s, t = mx_kscale(MID), mx_kscale(MID)
    return {"x": bf(np.random.standard_normal((B, D))),
            "h3": bf(np.maximum(np.random.standard_normal((B, MID)), 0.0) * s),
            "W4": bf(np.random.standard_normal((MID, MID)) * np.sqrt(2.0 / MID) / s[:, None] * t),
            "b4": bf(np.random.standard_normal(MID) * 0.2 * t),
            "W5": bf(np.random.standard_normal((MID, HALF)) * np.sqrt(2.0 / MID) / t[:, None]),
            "b5": bf(np.random.standard_normal(HALF) * 0.2)}


def reference(x, h3, W4, b4, W5, b5):
    x = f64(x)
    even = x[:, 0::2]
    odd = x[:, 1::2]
    h4 = np.maximum((mxq(f64(h3), 1, "e4m3") @ mxq(f64(W4), 0, "e4m3")) + f64(b4), 0.0)
    m = (mxq(h4, 1, "e4m3") @ mxq(f64(W5), 0, "e4m3")) + f64(b5)
    transformed = even + m
    return np.stack([transformed, odd], axis=2).reshape(B, -1)

@@ -1,0 +1,222 @@
+from contextlib import ExitStack
+
+import concourse.mybir as mybir
+from concourse.masks import make_identity
+
+FP8X4 = mybir.dt.float8_e4m3fn_x4
+BF16 = mybir.dt.bfloat16
+F32 = mybir.dt.float32
+U32 = mybir.dt.uint32
+U8 = mybir.dt.uint8
+ADD = mybir.AluOpType.add
+RELU = mybir.ActivationFunctionType.Relu
+
+P = 128
+B, HALF, MID = 8192, 128, 512
+UNITS = [1, 1, 2] + [4] * 14 + [2, 1, 1]
+NU = len(UNITS)
+NZ = 3
+S_SHARE = 4
+AHEAD = 5
+
+FLOPS = 2 * B * MID * (MID + HALF)
+
+
+def regroup(eng_copy, dst, src):
+    eng_copy(
+        out=dst.rearrange("p (c i) t -> p c t i", i=4),
+        in_=src.rearrange("p t (c i) -> p c t i", i=4),
+    )
+
+
+def tile_additivecoupling_pa_t_kernel(tc, x, h3, W4, b4, W5, b5, out):
+    nc = tc.nc
+    assert sum(UNITS) * P == B
+    row0 = [P * sum(UNITS[:u]) for u in range(NU)]
+    with ExitStack() as ctx:
+        const = ctx.enter_context(tc.tile_pool(name="const", bufs=1))
+        inp = ctx.enter_context(tc.tile_pool(name="inp", bufs=AHEAD + 3))
+        work = ctx.enter_context(tc.tile_pool(name="work", bufs=3))
+        outp = ctx.enter_context(tc.tile_pool(name="outp", bufs=4))
+        ps_t = ctx.enter_context(tc.psum_pool(name="ps_t", bufs=2))
+        ps_h = ctx.enter_context(tc.psum_pool(name="ps_h", bufs=4))
+        ps_o = ctx.enter_context(tc.psum_pool(name="ps_o", bufs=2))
+
+        h3_t = {}
+        x_t = {}
+
+        def load_h(u):
+            nt = UNITS[u]
+            ht = inp.tile([P, 4 * MID], BF16, name="ht", tag="ht")
+            nc.sync.dma_start(
+                out=ht[:, : nt * MID],
+                in_=h3[row0[u] : row0[u] + nt * P, :].rearrange("(p i) k -> p (i k)", i=nt),
+            )
+            h3_t[u] = ht
+
+        def load_x(u):
+            nt = UNITS[u]
+            xt = inp.tile([P, 4 * 2 * HALF], BF16, name="xt", tag="xt")
+            nc.sync.dma_start(
+                out=xt[:, : nt * 2 * HALF],
+                in_=x[row0[u] : row0[u] + nt * P, :].rearrange("(p i) c -> p (i c)", i=nt),
+            )
+            x_t[u] = xt
+
+        load_h(0)
+        bz = const.tile([P, P], BF16)
+        nc.vector.memset(bz[:], 0.0)
+        nc.scalar.dma_start(out=bz[0:4, :], in_=b4.rearrange("(t p) -> t p", p=P))
+        w4raw = const.tile([P, 4, MID], BF16)
+        nc.scalar.dma_start(
+            out=w4raw[:].rearrange("p (u e) n -> p u e n", u=2),
+            in_=W4.rearrange("(u p e) n -> p u e n", u=2, e=2),
+        )
+        w5raw = const.tile([P, 4, HALF], BF16)
+        nc.scalar.dma_start(out=w5raw[:], in_=W5.rearrange("(t p) n -> p t n", p=P))
+        b5bc = const.tile([P, HALF], BF16)
+        nc.scalar.dma_start(out=b5bc[:], in_=b5.partition_broadcast(P))
+        for u in range(1, AHEAD):
+            load_h(u)
+        for u in range(0, AHEAD - 2):
+            load_x(u)
+
+        ident_f = const.tile([P, P], F32)
+        make_identity(nc, ident_f[:])
+        ident_b = const.tile([P, P], BF16)
+        make_identity(nc, ident_b[:])
+
+        c3_t = {}
+        s3_t = {}
+        c4_t = {}
+        s4_t = {}
+
+        def stage_t(u):
+            nt = UNITS[u]
+            w = nt * P
+            hw = h3_t[u][:].bitcast(F32)
+            g3 = work.tile([P, 16 * P], BF16, name="g3", tag="g3", align_bytes=64)
+            g3w = g3[:].bitcast(F32)
+            for i0 in range(0, nt, 2):
+                n2 = min(2, nt - i0)
+                tp = ps_t.tile([P, 2, 2 * P], F32, name="tp", tag="tp")
+                for ii in range(n2):
+                    for u2 in range(2):
+                        c0 = 256 * (i0 + ii) + P * u2
+                        nc.tensor.transpose(
+                            tp[:, u2, ii * P : (ii + 1) * P], hw[:, c0 : c0 + P], ident_f[:]
+                        )
+                nc.scalar.copy(
+                    out=g3w[:, 256 * i0 : 256 * (i0 + n2)].rearrange("p (r u) -> p r u", u=2),
+                    in_=tp[:, :, : n2 * P].rearrange("p u r -> p r u"),
+                )
+            c3 = work.tile([P, 4 * P], U32, name="c3", tag="c3", align_bytes=64)
+            s3 = work.tile([P, 4 * P], U8, name="s3", tag="s3", align_bytes=64)
+            nc.vector.quantize_mx(
+                out=c3[:, :w].bitcast(FP8X4), scales=s3[:, :w], in_=g3[:, : 4 * w]
+            )
+            c3_t[u] = c3
+            s3_t[u] = s3
+
+        def stage_1(u):
+            w = UNITS[u] * P
+            h4p = work.tile([P, 4, 4 * P], BF16, name="h4p", tag="h4p")
+            for t in range(4):
+                hb = ps_h.tile([P, 4 * P], F32, name="hb", tag="hb")
+                nc.tensor.matmul_mx(
+                    out=hb[:, :w],
+                    lhsT=w4c[:, t * P : (t + 1) * P].bitcast(FP8X4),
+                    lhsT_scale=w4s[:, t * P : (t + 1) * P],
+                    rhs=c3_t[u][:, :w].bitcast(FP8X4),
+                    rhs_scale=s3_t[u][:, :w],
+                    start=True,
+                    stop=True,
+                )
+                nc.scalar.activation(
+                    out=h4p[:, t, :w], in_=hb[:, :w], func=RELU, bias=b4col[:, t : t + 1], scale=1.0
+                )
+            g4 = work.tile([P, 4 * P, 4], BF16, name="g4", tag="g4", align_bytes=64)
+            ws = w // S_SHARE
+            regroup(nc.scalar.copy, g4[:, :ws, :], h4p[:, :, :ws])
+            regroup(nc.vector.tensor_copy, g4[:, ws:w, :], h4p[:, :, ws:w])
+            c4 = work.tile([P, 4 * P], U32, name="c4", tag="c4", align_bytes=64)
+            s4 = work.tile([P, 4 * P], U8, name="s4", tag="s4", align_bytes=64)
+            nc.vector.quantize_mx(
+                out=c4[:, :w].bitcast(FP8X4),
+                scales=s4[:, :w],
+                in_=g4[:, :w, :].rearrange("p c t -> p (c t)"),
+            )
+            c4_t[u] = c4
+            s4_t[u] = s4
+
+        def stage_2(u):
+            nt = UNITS[u]
+            w = nt * P
+            ob = ps_o.tile([P, 4, HALF], F32, name="ob", tag="ob")
+            for i in range(nt):
+                nc.tensor.matmul_mx(
+                    out=ob[:, i, :],
+                    lhsT=c4_t[u][:, i * P : (i + 1) * P].bitcast(FP8X4),
+                    lhsT_scale=s4_t[u][:, i * P : (i + 1) * P],
+                    rhs=w5c[:].bitcast(FP8X4),
+                    rhs_scale=w5s[:],
+                    start=True,
+                    stop=True,
+                )
+            zt = z2[u % NZ]
+            nc.vector.tensor_tensor(
+                out=zt[:, 0, :w].rearrange("p (i j) -> p i j", i=nt),
+                in0=ob[:, :nt, :],
+                in1=b5bc[:].unsqueeze(1).to_broadcast([P, nt, HALF]),
+                op=ADD,
+            )
+            ot = outp.tile([P, 4 * 2 * HALF], F32, name="ot", tag="ot")
+            nc.vector.tensor_tensor(
+                out=ot[:, : 2 * w].rearrange("p (q e) -> p q e", e=2),
+                in0=x_t[u][:, : 2 * w].rearrange("p (q e) -> p q e", e=2),
+                in1=zt[:, :, :w].rearrange("p e q -> p q e"),
+                op=ADD,
+            )
+            nc.sync.dma_start(
+                out=out[row0[u] : row0[u] + w, :].rearrange("(p i) c -> p (i c)", i=nt),
+                in_=ot[:, : 2 * w],
+            )
+
+        stage_t(0)
+        z2 = []
+        for j in range(NZ):
+            zt = const.tile([P, 2, 4 * P], F32, name="z2_%d" % j)
+            nc.vector.memset(zt[:, 1, :], 0.0)
+            z2.append(zt)
+
+        w4g = const.tile([P, MID, 4], BF16, align_bytes=64)
+        regroup(nc.vector.tensor_copy, w4g[:], w4raw[:])
+        w4c = const.tile([P, MID], U32, align_bytes=64)
+        w4s = const.tile([P, MID], U8, align_bytes=64)
+        nc.vector.quantize_mx(
+            out=w4c[:].bitcast(FP8X4), scales=w4s[:], in_=w4g[:].rearrange("p c t -> p (c t)")
+        )
+        w5g = const.tile([P, HALF, 4], BF16, align_bytes=64)
+        regroup(nc.vector.tensor_copy, w5g[:], w5raw[:])
+        w5c = const.tile([P, HALF], U32, align_bytes=64)
+        w5s = const.tile([P, HALF], U8, align_bytes=64)
+        nc.vector.quantize_mx(
+            out=w5c[:].bitcast(FP8X4), scales=w5s[:], in_=w5g[:].rearrange("p c t -> p (c t)")
+        )
+
+        bt = ps_t.tile([P, P], BF16, name="bt", tag="tp")
+        nc.tensor.transpose(bt[:], bz[:], ident_b[:])
+        b4col = const.tile([P, 4], F32)
+        nc.vector.tensor_copy(out=b4col[:], in_=bt[:, 0:4])
+
+        for s in range(NU + 2):
+            if s + AHEAD < NU:
+                load_h(s + AHEAD)
+            if AHEAD - 2 <= s + AHEAD - 2 < NU:
+                load_x(s + AHEAD - 2)
+            if 0 < s < NU:
+                stage_t(s)
+            if 0 <= s - 1 < NU:
+                stage_1(s - 1)
+            if 0 <= s - 2 < NU:
+                stage_2(s - 2)

@@ -9,17 +9,26 @@ F32 = mybir.dt.float32
 U32 = mybir.dt.uint32
 U8 = mybir.dt.uint8
 ADD = mybir.AluOpType.add
+MAX = mybir.AluOpType.max
 RELU = mybir.ActivationFunctionType.Relu
 
 P = 128
 B, HALF, MID = 8192, 128, 512
-UNITS = [1, 1, 2] + [4] * 14 + [2, 1, 1]
+UNITS = [1,1,2,4,4,4,4,4,4,4,4,4,4,4,4,4,4,2,1,1]
 NU = len(UNITS)
 NZ = 3
-S_SHARE = 4
-AHEAD = 5
+MANUAL = True
 
 FLOPS = 2 * B * MID * (MID + HALF)
+
+
+def s_cols(u):
+    w = UNITS[u] * P
+    return (0 if u < 4 else (w if u >= NU - 4 else 3 * w // 16))
+
+
+def on_vector(kind, u, j):
+    return kind == "h" and u < 4 and j % 2 == 1
 
 
 def regroup(eng_copy, dst, src):
@@ -35,15 +44,16 @@ def tile_additivecoupling_pa_t_kernel(tc, x, h3, W4, b4, W5, b5, out):
     row0 = [P * sum(UNITS[:u]) for u in range(NU)]
     with ExitStack() as ctx:
         const = ctx.enter_context(tc.tile_pool(name="const", bufs=1))
-        inp = ctx.enter_context(tc.tile_pool(name="inp", bufs=AHEAD + 3))
+        inp = ctx.enter_context(tc.tile_pool(name="inp", bufs=8))
         work = ctx.enter_context(tc.tile_pool(name="work", bufs=3))
         outp = ctx.enter_context(tc.tile_pool(name="outp", bufs=4))
         ps_t = ctx.enter_context(tc.psum_pool(name="ps_t", bufs=2))
         ps_h = ctx.enter_context(tc.psum_pool(name="ps_h", bufs=4))
         ps_o = ctx.enter_context(tc.psum_pool(name="ps_o", bufs=2))
+        if MANUAL:
+            ctx.enter_context(tc.manual_schedule())
 
-        h3_t = {}
-        x_t = {}
+        live = {}
 
         def load_h(u):
             nt = UNITS[u]
@@ -52,7 +62,7 @@ def tile_additivecoupling_pa_t_kernel(tc, x, h3, W4, b4, W5, b5, out):
                 out=ht[:, : nt * MID],
                 in_=h3[row0[u] : row0[u] + nt * P, :].rearrange("(p i) k -> p (i k)", i=nt),
             )
-            h3_t[u] = ht
+            live["ht", u] = ht
 
         def load_x(u):
             nt = UNITS[u]
@@ -61,44 +71,58 @@ def tile_additivecoupling_pa_t_kernel(tc, x, h3, W4, b4, W5, b5, out):
                 out=xt[:, : nt * 2 * HALF],
                 in_=x[row0[u] : row0[u] + nt * P, :].rearrange("(p i) c -> p (i c)", i=nt),
             )
-            x_t[u] = xt
+            live["xt", u] = xt
 
-        load_h(0)
         bz = const.tile([P, P], BF16)
         nc.vector.memset(bz[:], 0.0)
-        nc.scalar.dma_start(out=bz[0:4, :], in_=b4.rearrange("(t p) -> t p", p=P))
         w4raw = const.tile([P, 4, MID], BF16)
         nc.scalar.dma_start(
             out=w4raw[:].rearrange("p (u e) n -> p u e n", u=2),
             in_=W4.rearrange("(u p e) n -> p u e n", u=2, e=2),
         )
+        nc.scalar.dma_start(out=bz[0:4, :], in_=b4.rearrange("(t p) -> t p", p=P))
         w5raw = const.tile([P, 4, HALF], BF16)
         nc.scalar.dma_start(out=w5raw[:], in_=W5.rearrange("(t p) n -> p t n", p=P))
         b5bc = const.tile([P, HALF], BF16)
         nc.scalar.dma_start(out=b5bc[:], in_=b5.partition_broadcast(P))
-        for u in range(1, AHEAD):
-            load_h(u)
-        for u in range(0, AHEAD - 2):
-            load_x(u)
-
         ident_f = const.tile([P, P], F32)
         make_identity(nc, ident_f[:])
         ident_b = const.tile([P, P], BF16)
         make_identity(nc, ident_b[:])
+        z2 = []
+        for j in range(NZ):
+            zt = const.tile([P, 2, 4 * P], F32, name="z2_%d" % j)
+            nc.vector.memset(zt[:, 1, :], 0.0)
+            z2.append(zt)
+        w4g = const.tile([P, MID, 4], BF16, align_bytes=64)
+        w4c = const.tile([P, MID], U32, align_bytes=64)
+        w4s = const.tile([P, MID], U8, align_bytes=64)
+        w5g = const.tile([P, HALF, 4], BF16, align_bytes=64)
+        w5c = const.tile([P, HALF], U32, align_bytes=64)
+        w5s = const.tile([P, HALF], U8, align_bytes=64)
+        b4col = const.tile([P, 4], F32)
 
-        c3_t = {}
-        s3_t = {}
-        c4_t = {}
-        s4_t = {}
+        def prep():
+            h = MID // 2
+            regroup(nc.vector.tensor_copy, w4g[:, :h, :], w4raw[:, :, :h])
+            regroup(nc.scalar.copy, w4g[:, h:, :], w4raw[:, :, h:])
+            bt = ps_o.tile([P, P], BF16, name="bt", tag="ob")
+            nc.tensor.transpose(bt[:], bz[:], ident_b[:])
+            regroup(nc.vector.tensor_copy, w5g[:], w5raw[:])
+            nc.vector.quantize_mx(
+                out=w4c[:].bitcast(FP8X4), scales=w4s[:], in_=w4g[:].rearrange("p c t -> p (c t)")
+            )
+            nc.vector.tensor_copy(out=b4col[:], in_=bt[:, 0:4])
+            nc.vector.quantize_mx(
+                out=w5c[:].bitcast(FP8X4), scales=w5s[:], in_=w5g[:].rearrange("p c t -> p (c t)")
+            )
 
-        def stage_t(u):
-            nt = UNITS[u]
-            w = nt * P
-            hw = h3_t[u][:].bitcast(F32)
-            g3 = work.tile([P, 16 * P], BF16, name="g3", tag="g3", align_bytes=64)
-            g3w = g3[:].bitcast(F32)
-            for i0 in range(0, nt, 2):
-                n2 = min(2, nt - i0)
+        def groups(u):
+            return [(i0, min(2, UNITS[u] - i0)) for i0 in range(0, UNITS[u], 2)]
+
+        def t_tr(u):
+            hw = live["ht", u][:].bitcast(F32)
+            for g, (i0, n2) in enumerate(groups(u)):
                 tp = ps_t.tile([P, 2, 2 * P], F32, name="tp", tag="tp")
                 for ii in range(n2):
                     for u2 in range(2):
@@ -106,117 +130,155 @@ def tile_additivecoupling_pa_t_kernel(tc, x, h3, W4, b4, W5, b5, out):
                         nc.tensor.transpose(
                             tp[:, u2, ii * P : (ii + 1) * P], hw[:, c0 : c0 + P], ident_f[:]
                         )
-                nc.scalar.copy(
+                live["tp", u, g] = tp
+
+        def t_ev(u):
+            g3 = work.tile([P, 16 * P], BF16, name="g3", tag="g3", align_bytes=64)
+            g3w = g3[:].bitcast(F32)
+            for g, (i0, n2) in enumerate(groups(u)):
+                cp = nc.vector.tensor_copy if on_vector("t", u, g) else nc.scalar.copy
+                cp(
                     out=g3w[:, 256 * i0 : 256 * (i0 + n2)].rearrange("p (r u) -> p r u", u=2),
-                    in_=tp[:, :, : n2 * P].rearrange("p u r -> p r u"),
+                    in_=live["tp", u, g][:, :, : n2 * P].rearrange("p u r -> p r u"),
                 )
+            live["g3", u] = g3
+
+        def q3(u):
+            w = UNITS[u] * P
             c3 = work.tile([P, 4 * P], U32, name="c3", tag="c3", align_bytes=64)
             s3 = work.tile([P, 4 * P], U8, name="s3", tag="s3", align_bytes=64)
             nc.vector.quantize_mx(
-                out=c3[:, :w].bitcast(FP8X4), scales=s3[:, :w], in_=g3[:, : 4 * w]
+                out=c3[:, :w].bitcast(FP8X4), scales=s3[:, :w], in_=live["g3", u][:, : 4 * w]
             )
-            c3_t[u] = c3
-            s3_t[u] = s3
+            live["c3", u] = c3
+            live["s3", u] = s3
 
-        def stage_1(u):
+        def mx1(u, t):
             w = UNITS[u] * P
-            h4p = work.tile([P, 4, 4 * P], BF16, name="h4p", tag="h4p")
-            for t in range(4):
-                hb = ps_h.tile([P, 4 * P], F32, name="hb", tag="hb")
-                nc.tensor.matmul_mx(
-                    out=hb[:, :w],
-                    lhsT=w4c[:, t * P : (t + 1) * P].bitcast(FP8X4),
-                    lhsT_scale=w4s[:, t * P : (t + 1) * P],
-                    rhs=c3_t[u][:, :w].bitcast(FP8X4),
-                    rhs_scale=s3_t[u][:, :w],
-                    start=True,
-                    stop=True,
+            hb = ps_h.tile([P, 4 * P], F32, name="hb", tag="hb")
+            nc.tensor.matmul_mx(
+                out=hb[:, :w],
+                lhsT=w4c[:, t * P : (t + 1) * P].bitcast(FP8X4),
+                lhsT_scale=w4s[:, t * P : (t + 1) * P],
+                rhs=live["c3", u][:, :w].bitcast(FP8X4),
+                rhs_scale=live["s3", u][:, :w],
+                start=True,
+                stop=True,
+            )
+            live["hb", u, t] = hb
+
+        def h_ev(u, t):
+            w = UNITS[u] * P
+            if t == 0:
+                live["h4p", u] = work.tile([P, 4, 4 * P], BF16, name="h4p", tag="h4p")
+            h4p = live["h4p", u]
+            hb = live["hb", u, t]
+            if on_vector("h", u, t):
+                nc.vector.tensor_scalar(
+                    out=h4p[:, t, :w], in0=hb[:, :w], scalar1=b4col[:, t : t + 1], scalar2=0.0,
+                    op0=ADD, op1=MAX,
                 )
+            else:
                 nc.scalar.activation(
                     out=h4p[:, t, :w], in_=hb[:, :w], func=RELU, bias=b4col[:, t : t + 1], scale=1.0
                 )
-            g4 = work.tile([P, 4 * P, 4], BF16, name="g4", tag="g4", align_bytes=64)
-            ws = w // S_SHARE
-            regroup(nc.scalar.copy, g4[:, :ws, :], h4p[:, :, :ws])
-            regroup(nc.vector.tensor_copy, g4[:, ws:w, :], h4p[:, :, ws:w])
+
+        def r_s(u):
+            live["g4", u] = work.tile([P, 4 * P, 4], BF16, name="g4", tag="g4", align_bytes=64)
+            ws = s_cols(u)
+            if ws > 0:
+                regroup(nc.scalar.copy, live["g4", u][:, :ws, :], live["h4p", u][:, :, :ws])
+
+        def r_v(u):
+            w = UNITS[u] * P
+            ws = s_cols(u)
+            if ws < w:
+                regroup(nc.vector.tensor_copy, live["g4", u][:, ws:w, :], live["h4p", u][:, :, ws:w])
+
+        def q4(u):
+            w = UNITS[u] * P
             c4 = work.tile([P, 4 * P], U32, name="c4", tag="c4", align_bytes=64)
             s4 = work.tile([P, 4 * P], U8, name="s4", tag="s4", align_bytes=64)
             nc.vector.quantize_mx(
                 out=c4[:, :w].bitcast(FP8X4),
                 scales=s4[:, :w],
-                in_=g4[:, :w, :].rearrange("p c t -> p (c t)"),
+                in_=live["g4", u][:, :w, :].rearrange("p c t -> p (c t)"),
             )
-            c4_t[u] = c4
-            s4_t[u] = s4
+            live["c4", u] = c4
+            live["s4", u] = s4
 
-        def stage_2(u):
-            nt = UNITS[u]
-            w = nt * P
+        def mx2(u):
             ob = ps_o.tile([P, 4, HALF], F32, name="ob", tag="ob")
-            for i in range(nt):
+            for i in range(UNITS[u]):
                 nc.tensor.matmul_mx(
                     out=ob[:, i, :],
-                    lhsT=c4_t[u][:, i * P : (i + 1) * P].bitcast(FP8X4),
-                    lhsT_scale=s4_t[u][:, i * P : (i + 1) * P],
+                    lhsT=live["c4", u][:, i * P : (i + 1) * P].bitcast(FP8X4),
+                    lhsT_scale=live["s4", u][:, i * P : (i + 1) * P],
                     rhs=w5c[:].bitcast(FP8X4),
                     rhs_scale=w5s[:],
                     start=True,
                     stop=True,
                 )
-            zt = z2[u % NZ]
+            live["ob", u] = ob
+
+        def mb(u):
+            nt = UNITS[u]
             nc.vector.tensor_tensor(
-                out=zt[:, 0, :w].rearrange("p (i j) -> p i j", i=nt),
-                in0=ob[:, :nt, :],
+                out=z2[u % NZ][:, 0, : nt * P].rearrange("p (i j) -> p i j", i=nt),
+                in0=live["ob", u][:, :nt, :],
                 in1=b5bc[:].unsqueeze(1).to_broadcast([P, nt, HALF]),
                 op=ADD,
             )
+
+        def fin(u):
+            w = UNITS[u] * P
             ot = outp.tile([P, 4 * 2 * HALF], F32, name="ot", tag="ot")
             nc.vector.tensor_tensor(
                 out=ot[:, : 2 * w].rearrange("p (q e) -> p q e", e=2),
-                in0=x_t[u][:, : 2 * w].rearrange("p (q e) -> p q e", e=2),
-                in1=zt[:, :, :w].rearrange("p e q -> p q e"),
+                in0=live["xt", u][:, : 2 * w].rearrange("p (q e) -> p q e", e=2),
+                in1=z2[u % NZ][:, :, :w].rearrange("p e q -> p q e"),
                 op=ADD,
             )
+            live["ot", u] = ot
+
+        def store(u):
+            nt = UNITS[u]
             nc.sync.dma_start(
-                out=out[row0[u] : row0[u] + w, :].rearrange("(p i) c -> p (i c)", i=nt),
-                in_=ot[:, : 2 * w],
+                out=out[row0[u] : row0[u] + nt * P, :].rearrange("(p i) c -> p (i c)", i=nt),
+                in_=live["ot", u][:, : nt * 2 * HALF],
             )
 
-        stage_t(0)
-        z2 = []
-        for j in range(NZ):
-            zt = const.tile([P, 2, 4 * P], F32, name="z2_%d" % j)
-            nc.vector.memset(zt[:, 1, :], 0.0)
-            z2.append(zt)
+        def ok(u):
+            return 0 <= u < NU
 
-        w4g = const.tile([P, MID, 4], BF16, align_bytes=64)
-        regroup(nc.vector.tensor_copy, w4g[:], w4raw[:])
-        w4c = const.tile([P, MID], U32, align_bytes=64)
-        w4s = const.tile([P, MID], U8, align_bytes=64)
-        nc.vector.quantize_mx(
-            out=w4c[:].bitcast(FP8X4), scales=w4s[:], in_=w4g[:].rearrange("p c t -> p (c t)")
-        )
-        w5g = const.tile([P, HALF, 4], BF16, align_bytes=64)
-        regroup(nc.vector.tensor_copy, w5g[:], w5raw[:])
-        w5c = const.tile([P, HALF], U32, align_bytes=64)
-        w5s = const.tile([P, HALF], U8, align_bytes=64)
-        nc.vector.quantize_mx(
-            out=w5c[:].bitcast(FP8X4), scales=w5s[:], in_=w5g[:].rearrange("p c t -> p (c t)")
-        )
-
-        bt = ps_t.tile([P, P], BF16, name="bt", tag="tp")
-        nc.tensor.transpose(bt[:], bz[:], ident_b[:])
-        b4col = const.tile([P, 4], F32)
-        nc.vector.tensor_copy(out=b4col[:], in_=bt[:, 0:4])
-
-        for s in range(NU + 2):
-            if s + AHEAD < NU:
-                load_h(s + AHEAD)
-            if AHEAD - 2 <= s + AHEAD - 2 < NU:
-                load_x(s + AHEAD - 2)
-            if 0 < s < NU:
-                stage_t(s)
-            if 0 <= s - 1 < NU:
-                stage_1(s - 1)
-            if 0 <= s - 2 < NU:
-                stage_2(s - 2)
+        for n in range(-5, NU + 5):
+            if ok(n + 5):
+                load_h(n + 5)
+            if ok(n + 1):
+                load_x(n + 1)
+            if ok(n - 4):
+                mx2(n - 4)
+            if ok(n):
+                t_ev(n)
+            if n == 0:
+                prep()
+            if ok(n + 1):
+                t_tr(n + 1)
+            if ok(n - 1):
+                q3(n - 1)
+            for t in range(4):
+                if ok(n - 2):
+                    h_ev(n - 2, t)
+                if ok(n - 1):
+                    mx1(n - 1, t)
+            if ok(n - 2):
+                r_s(n - 2)
+            if ok(n - 3):
+                r_v(n - 3)
+            if ok(n - 4):
+                mb(n - 4)
+            if ok(n - 3):
+                q4(n - 3)
+            if ok(n - 4):
+                fin(n - 4)
+                store(n - 4)

@@ -24,7 +24,7 @@ FLOPS = 2 * B * MID * (MID + HALF)
 
 def s_cols(u):
     w = UNITS[u] * P
-    return (0 if u < 4 else (w if u >= NU - 4 else 3 * w // 16))
+    return (w if u >= NU - 4 else 0)
 
 
 def on_vector(kind, u, j):

@@ -11,12 +11,12 @@ U8 = mybir.dt.uint8
 ADD = mybir.AluOpType.add
 MAX = mybir.AluOpType.max
 RELU = mybir.ActivationFunctionType.Relu
+IDENT = mybir.ActivationFunctionType.Identity
 
 P = 128
 B, HALF, MID = 8192, 128, 512
 UNITS = [1,1,2,4,4,4,4,4,4,4,4,4,4,4,4,4,4,2,1,1]
 NU = len(UNITS)
-NZ = 3
 MANUAL = True
 
 FLOPS = 2 * B * MID * (MID + HALF)
@@ -28,7 +28,7 @@ def s_cols(u):
 
 
 def on_vector(kind, u, j):
-    return kind == "h" and u < 4 and j % 2 == 1
+    return (kind == "h" and u < 4 and j % 2 == 1) or (kind == "t" and j == 1 and u % 2 == 1)
 
 
 def regroup(eng_copy, dst, src):
@@ -83,24 +83,21 @@ def tile_additivecoupling_pa_t_kernel(tc, x, h3, W4, b4, W5, b5, out):
         nc.scalar.dma_start(out=bz[0:4, :], in_=b4.rearrange("(t p) -> t p", p=P))
         w5raw = const.tile([P, 4, HALF], BF16)
         nc.scalar.dma_start(out=w5raw[:], in_=W5.rearrange("(t p) n -> p t n", p=P))
-        b5bc = const.tile([P, HALF], BF16)
-        nc.scalar.dma_start(out=b5bc[:], in_=b5.partition_broadcast(P))
+        nc.scalar.dma_start(out=bz[4:5, :], in_=b5.rearrange("(o j) -> o j", o=1))
         ident_f = const.tile([P, P], F32)
         make_identity(nc, ident_f[:])
         ident_b = const.tile([P, P], BF16)
         make_identity(nc, ident_b[:])
-        z2 = []
-        for j in range(NZ):
-            zt = const.tile([P, 2, 4 * P], F32, name="z2_%d" % j)
-            nc.vector.memset(zt[:, 1, :], 0.0)
-            z2.append(zt)
+        spread = const.tile([P, HALF, 2], F32)
+        nc.vector.memset(spread[:], 0.0)
+        nc.vector.tensor_copy(out=spread[:, :, 0], in_=ident_f[:])
         w4g = const.tile([P, MID, 4], BF16, align_bytes=64)
         w4c = const.tile([P, MID], U32, align_bytes=64)
         w4s = const.tile([P, MID], U8, align_bytes=64)
         w5g = const.tile([P, HALF, 4], BF16, align_bytes=64)
         w5c = const.tile([P, HALF], U32, align_bytes=64)
         w5s = const.tile([P, HALF], U8, align_bytes=64)
-        b4col = const.tile([P, 4], F32)
+        b4col = const.tile([P, 8], F32)
 
         def prep():
             h = MID // 2
@@ -112,7 +109,7 @@ def tile_additivecoupling_pa_t_kernel(tc, x, h3, W4, b4, W5, b5, out):
             nc.vector.quantize_mx(
                 out=w4c[:].bitcast(FP8X4), scales=w4s[:], in_=w4g[:].rearrange("p c t -> p (c t)")
             )
-            nc.vector.tensor_copy(out=b4col[:], in_=bt[:, 0:4])
+            nc.vector.tensor_copy(out=b4col[:], in_=bt[:, 0:8])
             nc.vector.quantize_mx(
                 out=w5c[:].bitcast(FP8X4), scales=w5s[:], in_=w5g[:].rearrange("p c t -> p (c t)")
             )
@@ -208,38 +205,51 @@ def tile_additivecoupling_pa_t_kernel(tc, x, h3, W4, b4, W5, b5, out):
             live["s4", u] = s4
 
         def mx2(u):
-            ob = ps_o.tile([P, 4, HALF], F32, name="ob", tag="ob")
-            for i in range(UNITS[u]):
-                nc.tensor.matmul_mx(
-                    out=ob[:, i, :],
-                    lhsT=live["c4", u][:, i * P : (i + 1) * P].bitcast(FP8X4),
-                    lhsT_scale=live["s4", u][:, i * P : (i + 1) * P],
-                    rhs=w5c[:].bitcast(FP8X4),
-                    rhs_scale=w5s[:],
-                    start=True,
-                    stop=True,
-                )
-            live["ob", u] = ob
-
-        def mb(u):
-            nt = UNITS[u]
-            nc.vector.tensor_tensor(
-                out=z2[u % NZ][:, 0, : nt * P].rearrange("p (i j) -> p i j", i=nt),
-                in0=live["ob", u][:, :nt, :],
-                in1=b5bc[:].unsqueeze(1).to_broadcast([P, nt, HALF]),
-                op=ADD,
-            )
-
-        def fin(u):
             w = UNITS[u] * P
-            ot = outp.tile([P, 4 * 2 * HALF], F32, name="ot", tag="ot")
-            nc.vector.tensor_tensor(
-                out=ot[:, : 2 * w].rearrange("p (q e) -> p q e", e=2),
-                in0=live["xt", u][:, : 2 * w].rearrange("p (q e) -> p q e", e=2),
-                in1=z2[u % NZ][:, :, :w].rearrange("p e q -> p q e"),
-                op=ADD,
+            mt = ps_h.tile([P, 4 * P], F32, name="mt", tag="hb")
+            nc.tensor.matmul_mx(
+                out=mt[:, :w],
+                lhsT=w5c[:].bitcast(FP8X4),
+                lhsT_scale=w5s[:],
+                rhs=live["c4", u][:, :w].bitcast(FP8X4),
+                rhs_scale=live["s4", u][:, :w],
+                start=True,
+                stop=True,
             )
-            live["ot", u] = ot
+            live["mt", u] = mt
+
+        def m_ev(u):
+            w = UNITS[u] * P
+            mtb = work.tile([P, 4 * P], F32, name="mtb", tag="mtb")
+            nc.scalar.activation(
+                out=mtb[:, :w], in_=live["mt", u][:, :w], func=IDENT, bias=b4col[:, 4:5], scale=1.0
+            )
+            live["mtb", u] = mtb
+
+        def et_tr(u):
+            for g, (i0, n2) in enumerate(groups(u)):
+                ob = ps_o.tile([P, 2, 2 * HALF], F32, name="ob", tag="ob")
+                for ii in range(n2):
+                    for hf in range(2):
+                        nc.tensor.transpose(
+                            ob[:, ii, hf * P : (hf + 1) * P],
+                            live["mtb", u][:, (i0 + ii) * P : (i0 + ii + 1) * P],
+                            spread[:].rearrange("p j e -> p (j e)")[:, hf * P : (hf + 1) * P],
+                        )
+                live["ob", u, g] = ob
+
+        def i2(u, g):
+            if g == 0:
+                live["ot", u] = outp.tile([P, 4 * 2 * HALF], F32, name="ot", tag="ot")
+            if g < len(groups(u)):
+                i0, n2 = groups(u)[g]
+                cols = slice(i0 * 2 * HALF, (i0 + n2) * 2 * HALF)
+                nc.vector.tensor_tensor(
+                    out=live["ot", u][:, cols],
+                    in0=live["ob", u, g][:, :n2, :].rearrange("p i c -> p (i c)"),
+                    in1=live["xt", u][:, cols],
+                    op=ADD,
+                )
 
         def store(u):
             nt = UNITS[u]
@@ -251,13 +261,13 @@ def tile_additivecoupling_pa_t_kernel(tc, x, h3, W4, b4, W5, b5, out):
         def ok(u):
             return 0 <= u < NU
 
-        for n in range(-5, NU + 5):
+        for n in range(-5, NU + 6):
             if ok(n + 5):
                 load_h(n + 5)
             if ok(n + 1):
                 load_x(n + 1)
-            if ok(n - 4):
-                mx2(n - 4)
+            if ok(n - 5):
+                et_tr(n - 5)
             if ok(n):
                 t_ev(n)
             if n == 0:
@@ -266,19 +276,27 @@ def tile_additivecoupling_pa_t_kernel(tc, x, h3, W4, b4, W5, b5, out):
                 t_tr(n + 1)
             if ok(n - 1):
                 q3(n - 1)
-            for t in range(4):
+            if ok(n - 2):
+                h_ev(n - 2, 0)
+            if ok(n - 4):
+                mx2(n - 4)
+            for t in range(1, 4):
                 if ok(n - 2):
                     h_ev(n - 2, t)
                 if ok(n - 1):
-                    mx1(n - 1, t)
+                    mx1(n - 1, t - 1)
+            if ok(n - 4):
+                m_ev(n - 4)
+            if ok(n - 1):
+                mx1(n - 1, 3)
             if ok(n - 2):
                 r_s(n - 2)
             if ok(n - 3):
                 r_v(n - 3)
-            if ok(n - 4):
-                mb(n - 4)
+            if ok(n - 5):
+                i2(n - 5, 0)
             if ok(n - 3):
                 q4(n - 3)
-            if ok(n - 4):
-                fin(n - 4)
-                store(n - 4)
+            if ok(n - 5):
+                i2(n - 5, 1)
+                store(n - 5)

@@ -11,12 +11,12 @@ U8 = mybir.dt.uint8
 ADD = mybir.AluOpType.add
 MAX = mybir.AluOpType.max
 RELU = mybir.ActivationFunctionType.Relu
-IDENT = mybir.ActivationFunctionType.Identity
 
 P = 128
 B, HALF, MID = 8192, 128, 512
 UNITS = [1,1,2,4,4,4,4,4,4,4,4,4,4,4,4,4,4,2,1,1]
 NU = len(UNITS)
+NZ = 3
 MANUAL = True
 
 FLOPS = 2 * B * MID * (MID + HALF)
@@ -24,11 +24,11 @@ FLOPS = 2 * B * MID * (MID + HALF)
 
 def s_cols(u):
     w = UNITS[u] * P
-    return (w if u >= NU - 4 else 0)
+    return (0 if u < 4 else (w if u >= NU - 4 else 3 * w // 32))
 
 
 def on_vector(kind, u, j):
-    return (kind == "h" and u < 4 and j % 2 == 1) or (kind == "t" and j == 1 and u % 2 == 1)
+    return kind == "h" and u < 4 and j % 2 == 1
 
 
 def regroup(eng_copy, dst, src):
@@ -83,21 +83,24 @@ def tile_additivecoupling_pa_t_kernel(tc, x, h3, W4, b4, W5, b5, out):
         nc.scalar.dma_start(out=bz[0:4, :], in_=b4.rearrange("(t p) -> t p", p=P))
         w5raw = const.tile([P, 4, HALF], BF16)
         nc.scalar.dma_start(out=w5raw[:], in_=W5.rearrange("(t p) n -> p t n", p=P))
-        nc.scalar.dma_start(out=bz[4:5, :], in_=b5.rearrange("(o j) -> o j", o=1))
+        b5bc = const.tile([P, HALF], BF16)
+        nc.scalar.dma_start(out=b5bc[:], in_=b5.partition_broadcast(P))
         ident_f = const.tile([P, P], F32)
         make_identity(nc, ident_f[:])
         ident_b = const.tile([P, P], BF16)
         make_identity(nc, ident_b[:])
-        spread = const.tile([P, HALF, 2], F32)
-        nc.vector.memset(spread[:], 0.0)
-        nc.vector.tensor_copy(out=spread[:, :, 0], in_=ident_f[:])
+        z2 = []
+        for j in range(NZ):
+            zt = const.tile([P, 2, 4 * P], F32, name="z2_%d" % j)
+            nc.vector.memset(zt[:, 1, :], 0.0)
+            z2.append(zt)
         w4g = const.tile([P, MID, 4], BF16, align_bytes=64)
         w4c = const.tile([P, MID], U32, align_bytes=64)
         w4s = const.tile([P, MID], U8, align_bytes=64)
         w5g = const.tile([P, HALF, 4], BF16, align_bytes=64)
         w5c = const.tile([P, HALF], U32, align_bytes=64)
         w5s = const.tile([P, HALF], U8, align_bytes=64)
-        b4col = const.tile([P, 8], F32)
+        b4col = const.tile([P, 4], F32)
 
         def prep():
             h = MID // 2
@@ -109,7 +112,7 @@ def tile_additivecoupling_pa_t_kernel(tc, x, h3, W4, b4, W5, b5, out):
             nc.vector.quantize_mx(
                 out=w4c[:].bitcast(FP8X4), scales=w4s[:], in_=w4g[:].rearrange("p c t -> p (c t)")
             )
-            nc.vector.tensor_copy(out=b4col[:], in_=bt[:, 0:8])
+            nc.vector.tensor_copy(out=b4col[:], in_=bt[:, 0:4])
             nc.vector.quantize_mx(
                 out=w5c[:].bitcast(FP8X4), scales=w5s[:], in_=w5g[:].rearrange("p c t -> p (c t)")
             )
@@ -205,51 +208,38 @@ def tile_additivecoupling_pa_t_kernel(tc, x, h3, W4, b4, W5, b5, out):
             live["s4", u] = s4
 
         def mx2(u):
-            w = UNITS[u] * P
-            mt = ps_h.tile([P, 4 * P], F32, name="mt", tag="hb")
-            nc.tensor.matmul_mx(
-                out=mt[:, :w],
-                lhsT=w5c[:].bitcast(FP8X4),
-                lhsT_scale=w5s[:],
-                rhs=live["c4", u][:, :w].bitcast(FP8X4),
-                rhs_scale=live["s4", u][:, :w],
-                start=True,
-                stop=True,
-            )
-            live["mt", u] = mt
-
-        def m_ev(u):
-            w = UNITS[u] * P
-            mtb = work.tile([P, 4 * P], F32, name="mtb", tag="mtb")
-            nc.scalar.activation(
-                out=mtb[:, :w], in_=live["mt", u][:, :w], func=IDENT, bias=b4col[:, 4:5], scale=1.0
-            )
-            live["mtb", u] = mtb
-
-        def et_tr(u):
-            for g, (i0, n2) in enumerate(groups(u)):
-                ob = ps_o.tile([P, 2, 2 * HALF], F32, name="ob", tag="ob")
-                for ii in range(n2):
-                    for hf in range(2):
-                        nc.tensor.transpose(
-                            ob[:, ii, hf * P : (hf + 1) * P],
-                            live["mtb", u][:, (i0 + ii) * P : (i0 + ii + 1) * P],
-                            spread[:].rearrange("p j e -> p (j e)")[:, hf * P : (hf + 1) * P],
-                        )
-                live["ob", u, g] = ob
-
-        def i2(u, g):
-            if g == 0:
-                live["ot", u] = outp.tile([P, 4 * 2 * HALF], F32, name="ot", tag="ot")
-            if g < len(groups(u)):
-                i0, n2 = groups(u)[g]
-                cols = slice(i0 * 2 * HALF, (i0 + n2) * 2 * HALF)
-                nc.vector.tensor_tensor(
-                    out=live["ot", u][:, cols],
-                    in0=live["ob", u, g][:, :n2, :].rearrange("p i c -> p (i c)"),
-                    in1=live["xt", u][:, cols],
-                    op=ADD,
+            ob = ps_o.tile([P, 4, HALF], F32, name="ob", tag="ob")
+            for i in range(UNITS[u]):
+                nc.tensor.matmul_mx(
+                    out=ob[:, i, :],
+                    lhsT=live["c4", u][:, i * P : (i + 1) * P].bitcast(FP8X4),
+                    lhsT_scale=live["s4", u][:, i * P : (i + 1) * P],
+                    rhs=w5c[:].bitcast(FP8X4),
+                    rhs_scale=w5s[:],
+                    start=True,
+                    stop=True,
                 )
+            live["ob", u] = ob
+
+        def mb(u):
+            nt = UNITS[u]
+            nc.vector.tensor_tensor(
+                out=z2[u % NZ][:, 0, : nt * P].rearrange("p (i j) -> p i j", i=nt),
+                in0=live["ob", u][:, :nt, :],
+                in1=b5bc[:].unsqueeze(1).to_broadcast([P, nt, HALF]),
+                op=ADD,
+            )
+
+        def fin(u):
+            w = UNITS[u] * P
+            ot = outp.tile([P, 4 * 2 * HALF], F32, name="ot", tag="ot")
+            nc.vector.tensor_tensor(
+                out=ot[:, : 2 * w].rearrange("p (q e) -> p q e", e=2),
+                in0=live["xt", u][:, : 2 * w].rearrange("p (q e) -> p q e", e=2),
+                in1=z2[u % NZ][:, :, :w].rearrange("p e q -> p q e"),
+                op=ADD,
+            )
+            live["ot", u] = ot
 
         def store(u):
             nt = UNITS[u]
@@ -261,13 +251,13 @@ def tile_additivecoupling_pa_t_kernel(tc, x, h3, W4, b4, W5, b5, out):
         def ok(u):
             return 0 <= u < NU
 
-        for n in range(-5, NU + 6):
+        for n in range(-5, NU + 5):
             if ok(n + 5):
                 load_h(n + 5)
             if ok(n + 1):
                 load_x(n + 1)
-            if ok(n - 5):
-                et_tr(n - 5)
+            if ok(n - 4):
+                mx2(n - 4)
             if ok(n):
                 t_ev(n)
             if n == 0:
@@ -276,27 +266,19 @@ def tile_additivecoupling_pa_t_kernel(tc, x, h3, W4, b4, W5, b5, out):
                 t_tr(n + 1)
             if ok(n - 1):
                 q3(n - 1)
-            if ok(n - 2):
-                h_ev(n - 2, 0)
-            if ok(n - 4):
-                mx2(n - 4)
-            for t in range(1, 4):
+            for t in range(4):
                 if ok(n - 2):
                     h_ev(n - 2, t)
                 if ok(n - 1):
-                    mx1(n - 1, t - 1)
-            if ok(n - 4):
-                m_ev(n - 4)
-            if ok(n - 1):
-                mx1(n - 1, 3)
+                    mx1(n - 1, t)
             if ok(n - 2):
                 r_s(n - 2)
             if ok(n - 3):
                 r_v(n - 3)
-            if ok(n - 5):
-                i2(n - 5, 0)
+            if ok(n - 4):
+                mb(n - 4)
             if ok(n - 3):
                 q4(n - 3)
-            if ok(n - 5):
-                i2(n - 5, 1)
-                store(n - 5)
+            if ok(n - 4):
+                fin(n - 4)
+                store(n - 4)

@@ -9,26 +9,43 @@ F32 = mybir.dt.float32
 U32 = mybir.dt.uint32
 U8 = mybir.dt.uint8
 ADD = mybir.AluOpType.add
+MULT = mybir.AluOpType.mult
 MAX = mybir.AluOpType.max
 RELU = mybir.ActivationFunctionType.Relu
+IDENT = mybir.ActivationFunctionType.Identity
 
 P = 128
 B, HALF, MID = 8192, 128, 512
-UNITS = [1,1,2,4,4,4,4,4,4,4,4,4,4,4,4,4,4,2,1,1]
+UNITS = [2] + [4] * 15 + [1, 1]
 NU = len(UNITS)
-NZ = 3
-MANUAL = True
+G_SHARE = 24
+S_SHARE = 8
+EDGE = 2
+HEAD = 0
+TAIL_S = 0.5
+W4_V = 352
 
 FLOPS = 2 * B * MID * (MID + HALF)
 
 
+def edge(u):
+    return u < HEAD or u >= NU - EDGE
+
+
+def g_cols(u):
+    return 0 if edge(u) else 4 * G_SHARE * UNITS[u]
+
+
 def s_cols(u):
-    w = UNITS[u] * P
-    return (0 if u < 4 else (w if u >= NU - 4 else 3 * w // 32))
+    return 16 * round(UNITS[u] * P * TAIL_S / 16) if u >= NU - EDGE else (0 if edge(u) else 4 * S_SHARE * UNITS[u])
 
 
-def on_vector(kind, u, j):
-    return kind == "h" and u < 4 and j % 2 == 1
+def t_on_vector(u, g):
+    return True
+
+
+def h_on_vector(u, t):
+    return False
 
 
 def regroup(eng_copy, dst, src):
@@ -48,10 +65,10 @@ def tile_additivecoupling_pa_t_kernel(tc, x, h3, W4, b4, W5, b5, out):
         work = ctx.enter_context(tc.tile_pool(name="work", bufs=3))
         outp = ctx.enter_context(tc.tile_pool(name="outp", bufs=4))
         ps_t = ctx.enter_context(tc.psum_pool(name="ps_t", bufs=2))
-        ps_h = ctx.enter_context(tc.psum_pool(name="ps_h", bufs=4))
-        ps_o = ctx.enter_context(tc.psum_pool(name="ps_o", bufs=2))
-        if MANUAL:
-            ctx.enter_context(tc.manual_schedule())
+        ps_h = ctx.enter_context(tc.psum_pool(name="ps_h", bufs=3))
+        ps_m = ctx.enter_context(tc.psum_pool(name="ps_m", bufs=1))
+        ps_z = ctx.enter_context(tc.psum_pool(name="ps_z", bufs=1))
+        ctx.enter_context(tc.manual_schedule())
 
         live = {}
 
@@ -73,46 +90,54 @@ def tile_additivecoupling_pa_t_kernel(tc, x, h3, W4, b4, W5, b5, out):
             )
             live["xt", u] = xt
 
-        bz = const.tile([P, P], BF16)
+        bz = const.tile([P, 2 * P], BF16)
         nc.vector.memset(bz[:], 0.0)
+        zr = const.tile([P, 2 * P], BF16)
+        nc.vector.memset(zr[:], 0.0)
         w4raw = const.tile([P, 4, MID], BF16)
-        nc.scalar.dma_start(
+        load_h(0)
+        nc.sync.dma_start(out=bz[0:4, 0:P], in_=b4.rearrange("(t p) -> t p", p=P))
+        nc.sync.dma_start(out=bz[4:5, 0:P], in_=b5.unsqueeze(0))
+        nc.sync.dma_start(
             out=w4raw[:].rearrange("p (u e) n -> p u e n", u=2),
             in_=W4.rearrange("(u p e) n -> p u e n", u=2, e=2),
         )
-        nc.scalar.dma_start(out=bz[0:4, :], in_=b4.rearrange("(t p) -> t p", p=P))
         w5raw = const.tile([P, 4, HALF], BF16)
-        nc.scalar.dma_start(out=w5raw[:], in_=W5.rearrange("(t p) n -> p t n", p=P))
-        b5bc = const.tile([P, HALF], BF16)
-        nc.scalar.dma_start(out=b5bc[:], in_=b5.partition_broadcast(P))
+        load_h(1)
+        nc.sync.dma_start(out=w5raw[:], in_=W5.rearrange("(t p) n -> p t n", p=P))
         ident_f = const.tile([P, P], F32)
         make_identity(nc, ident_f[:])
         ident_b = const.tile([P, P], BF16)
         make_identity(nc, ident_b[:])
-        z2 = []
-        for j in range(NZ):
-            zt = const.tile([P, 2, 4 * P], F32, name="z2_%d" % j)
-            nc.vector.memset(zt[:, 1, :], 0.0)
-            z2.append(zt)
+        zz = [ps_z.tile([P, 2, 2 * P], F32, name="zz%d" % k) for k in range(2)]
         w4g = const.tile([P, MID, 4], BF16, align_bytes=64)
         w4c = const.tile([P, MID], U32, align_bytes=64)
         w4s = const.tile([P, MID], U8, align_bytes=64)
         w5g = const.tile([P, HALF, 4], BF16, align_bytes=64)
         w5c = const.tile([P, HALF], U32, align_bytes=64)
         w5s = const.tile([P, HALF], U8, align_bytes=64)
-        b4col = const.tile([P, 4], F32)
+        bcol = const.tile([P, 8], F32)
 
         def prep():
-            h = MID // 2
+            h = W4_V
             regroup(nc.vector.tensor_copy, w4g[:, :h, :], w4raw[:, :, :h])
             regroup(nc.scalar.copy, w4g[:, h:, :], w4raw[:, :, h:])
-            bt = ps_o.tile([P, P], BF16, name="bt", tag="ob")
-            nc.tensor.transpose(bt[:], bz[:], ident_b[:])
-            regroup(nc.vector.tensor_copy, w5g[:], w5raw[:])
+            q3(0)
             nc.vector.quantize_mx(
                 out=w4c[:].bitcast(FP8X4), scales=w4s[:], in_=w4g[:].rearrange("p c t -> p (c t)")
             )
-            nc.vector.tensor_copy(out=b4col[:], in_=bt[:, 0:4])
+            bt = ps_m.tile([P, P], BF16, name="bt", tag="mb")
+            nc.tensor.transpose(bt[:], bz[:, 0:P], ident_b[:])
+            for k in range(2):
+                nc.tensor.matmul(
+                    zz[k][:, 1, :], lhsT=zr[:, 0:P], rhs=zr[:], start=True, stop=True
+                )
+            nc.vector.tensor_copy(out=bcol[:], in_=bt[:, 0:8])
+
+        def prep5a():
+            regroup(nc.vector.tensor_copy, w5g[:], w5raw[:])
+
+        def prep5b():
             nc.vector.quantize_mx(
                 out=w5c[:].bitcast(FP8X4), scales=w5s[:], in_=w5g[:].rearrange("p c t -> p (c t)")
             )
@@ -132,16 +157,18 @@ def tile_additivecoupling_pa_t_kernel(tc, x, h3, W4, b4, W5, b5, out):
                         )
                 live["tp", u, g] = tp
 
-        def t_ev(u):
-            g3 = work.tile([P, 16 * P], BF16, name="g3", tag="g3", align_bytes=64)
-            g3w = g3[:].bitcast(F32)
+        def t_ev(u, vec):
+            if ("g3", u) not in live:
+                live["g3", u] = work.tile([P, 16 * P], BF16, name="g3", tag="g3", align_bytes=64)
+            g3w = live["g3", u][:].bitcast(F32)
             for g, (i0, n2) in enumerate(groups(u)):
-                cp = nc.vector.tensor_copy if on_vector("t", u, g) else nc.scalar.copy
+                if t_on_vector(u, g) != vec:
+                    continue
+                cp = nc.vector.tensor_copy if vec else nc.scalar.copy
                 cp(
                     out=g3w[:, 256 * i0 : 256 * (i0 + n2)].rearrange("p (r u) -> p r u", u=2),
                     in_=live["tp", u, g][:, :, : n2 * P].rearrange("p u r -> p r u"),
                 )
-            live["g3", u] = g3
 
         def q3(u):
             w = UNITS[u] * P
@@ -173,14 +200,14 @@ def tile_additivecoupling_pa_t_kernel(tc, x, h3, W4, b4, W5, b5, out):
                 live["h4p", u] = work.tile([P, 4, 4 * P], BF16, name="h4p", tag="h4p")
             h4p = live["h4p", u]
             hb = live["hb", u, t]
-            if on_vector("h", u, t):
+            if h_on_vector(u, t):
                 nc.vector.tensor_scalar(
-                    out=h4p[:, t, :w], in0=hb[:, :w], scalar1=b4col[:, t : t + 1], scalar2=0.0,
+                    out=h4p[:, t, :w], in0=hb[:, :w], scalar1=bcol[:, t : t + 1], scalar2=0.0,
                     op0=ADD, op1=MAX,
                 )
             else:
                 nc.scalar.activation(
-                    out=h4p[:, t, :w], in_=hb[:, :w], func=RELU, bias=b4col[:, t : t + 1], scale=1.0
+                    out=h4p[:, t, :w], in_=hb[:, :w], func=RELU, bias=bcol[:, t : t + 1], scale=1.0
                 )
 
         def r_s(u):
@@ -191,9 +218,22 @@ def tile_additivecoupling_pa_t_kernel(tc, x, h3, W4, b4, W5, b5, out):
 
         def r_v(u):
             w = UNITS[u] * P
-            ws = s_cols(u)
-            if ws < w:
-                regroup(nc.vector.tensor_copy, live["g4", u][:, ws:w, :], live["h4p", u][:, :, ws:w])
+            a = s_cols(u)
+            b = w - g_cols(u)
+            if a < b:
+                regroup(nc.vector.tensor_copy, live["g4", u][:, a:b, :], live["h4p", u][:, :, a:b])
+
+        def r_g(u):
+            w = UNITS[u] * P
+            n = g_cols(u)
+            if n > 0:
+                tok = work.tile([P, 1], F32, name="tok", tag="tok")
+                nc.vector.memset(tok[:], 1.0)
+                nc.gpsimd.tensor_scalar(
+                    out=live["g4", u][:, w - n : w, :],
+                    in0=live["h4p", u][:, :, w - n : w].rearrange("p t c -> p c t"),
+                    scalar1=tok[:], scalar2=0.0, op0=MULT, op1=ADD,
+                )
 
         def q4(u):
             w = UNITS[u] * P
@@ -208,77 +248,92 @@ def tile_additivecoupling_pa_t_kernel(tc, x, h3, W4, b4, W5, b5, out):
             live["s4", u] = s4
 
         def mx2(u):
-            ob = ps_o.tile([P, 4, HALF], F32, name="ob", tag="ob")
-            for i in range(UNITS[u]):
-                nc.tensor.matmul_mx(
-                    out=ob[:, i, :],
-                    lhsT=live["c4", u][:, i * P : (i + 1) * P].bitcast(FP8X4),
-                    lhsT_scale=live["s4", u][:, i * P : (i + 1) * P],
-                    rhs=w5c[:].bitcast(FP8X4),
-                    rhs_scale=w5s[:],
-                    start=True,
-                    stop=True,
-                )
-            live["ob", u] = ob
-
-        def mb(u):
-            nt = UNITS[u]
-            nc.vector.tensor_tensor(
-                out=z2[u % NZ][:, 0, : nt * P].rearrange("p (i j) -> p i j", i=nt),
-                in0=live["ob", u][:, :nt, :],
-                in1=b5bc[:].unsqueeze(1).to_broadcast([P, nt, HALF]),
-                op=ADD,
+            w = UNITS[u] * P
+            mb = ps_m.tile([P, 4 * P], F32, name="mb", tag="mb")
+            nc.tensor.matmul_mx(
+                out=mb[:, :w],
+                lhsT=w5c[:].bitcast(FP8X4),
+                lhsT_scale=w5s[:],
+                rhs=live["c4", u][:, :w].bitcast(FP8X4),
+                rhs_scale=live["s4", u][:, :w],
+                start=True,
+                stop=True,
             )
+            live["mb", u] = mb
+
+        def m_ev(u):
+            w = UNITS[u] * P
+            mt = work.tile([P, 4 * P], F32, name="mt", tag="mt")
+            nc.scalar.activation(
+                out=mt[:, :w], in_=live["mb", u][:, :w], func=IDENT, bias=bcol[:, 4:5], scale=1.0
+            )
+            live["mt", u] = mt
+
+        def m_tr(u):
+            for g, (i0, n2) in enumerate(groups(u)):
+                for ii in range(n2):
+                    nc.tensor.transpose(
+                        zz[g][:, 0, ii * P : (ii + 1) * P],
+                        live["mt", u][:, (i0 + ii) * P : (i0 + ii + 1) * P],
+                        ident_f[:],
+                    )
 
         def fin(u):
-            w = UNITS[u] * P
-            ot = outp.tile([P, 4 * 2 * HALF], F32, name="ot", tag="ot")
-            nc.vector.tensor_tensor(
-                out=ot[:, : 2 * w].rearrange("p (q e) -> p q e", e=2),
-                in0=live["xt", u][:, : 2 * w].rearrange("p (q e) -> p q e", e=2),
-                in1=z2[u % NZ][:, :, :w].rearrange("p e q -> p q e"),
-                op=ADD,
-            )
-            live["ot", u] = ot
-
-        def store(u):
             nt = UNITS[u]
+            ot = outp.tile([P, 4 * 2 * HALF], F32, name="ot", tag="ot")
+            for g, (i0, n2) in enumerate(groups(u)):
+                a, b = 2 * P * i0, 2 * P * (i0 + n2)
+                nc.vector.tensor_tensor(
+                    out=ot[:, a:b].rearrange("p (q e) -> p q e", e=2),
+                    in0=zz[g][:, :, : n2 * P].rearrange("p e q -> p q e"),
+                    in1=live["xt", u][:, a:b].rearrange("p (q e) -> p q e", e=2),
+                    op=ADD,
+                )
             nc.sync.dma_start(
                 out=out[row0[u] : row0[u] + nt * P, :].rearrange("(p i) c -> p (i c)", i=nt),
-                in_=live["ot", u][:, : nt * 2 * HALF],
+                in_=ot[:, : nt * 2 * HALF],
             )
 
         def ok(u):
             return 0 <= u < NU
 
-        for n in range(-5, NU + 5):
-            if ok(n + 5):
+        LF = 4
+        for n in range(-5, NU + 6):
+            if ok(n + 5) and n + 5 > 1:
                 load_h(n + 5)
             if ok(n + 1):
                 load_x(n + 1)
-            if ok(n - 4):
-                mx2(n - 4)
-            if ok(n):
-                t_ev(n)
             if n == 0:
+                t_ev(0, True)
+                t_ev(0, False)
                 prep()
-            if ok(n + 1):
-                t_tr(n + 1)
-            if ok(n - 1):
+            if ok(n - LF):
+                m_tr(n - LF)
+            if ok(n - 3):
+                q4(n - 3)
+            if ok(n - 1) and n > 1:
                 q3(n - 1)
-            for t in range(4):
-                if ok(n - 2):
-                    h_ev(n - 2, t)
-                if ok(n - 1):
-                    mx1(n - 1, t)
+            if ok(n - 3):
+                mx2(n - 3)
             if ok(n - 2):
                 r_s(n - 2)
             if ok(n - 3):
-                r_v(n - 3)
-            if ok(n - 4):
-                mb(n - 4)
-            if ok(n - 3):
-                q4(n - 3)
-            if ok(n - 4):
-                fin(n - 4)
-                store(n - 4)
+                m_ev(n - 3)
+            for t in range(4):
+                if ok(n - 1):
+                    mx1(n - 1, t)
+                    h_ev(n - 1, t)
+            if n == 1:
+                prep5a()
+            if ok(n - 2):
+                r_v(n - 2)
+                r_g(n - 2)
+            if ok(n) and n > 0:
+                t_ev(n, True)
+                t_ev(n, False)
+            if ok(n - LF):
+                fin(n - LF)
+            if n == 1:
+                prep5b()
+            if ok(n + 1):
+                t_tr(n + 1)

@@ -18,9 +18,10 @@ P = 128
 B, HALF, MID = 8192, 128, 512
 UNITS = [2] + [4] * 15 + [1, 1]
 NU = len(UNITS)
-G_SHARE = 24
+G_SHARE = 20
 S_SHARE = 8
 EDGE = 2
+RV = 1
 HEAD = 0
 TAIL_S = 0.5
 W4_V = 352
@@ -309,14 +310,19 @@ def tile_additivecoupling_pa_t_kernel(tc, x, h3, W4, b4, W5, b5, out):
                 prep()
             if ok(n - LF):
                 m_tr(n - LF)
-            if ok(n - 3):
-                q4(n - 3)
             if ok(n - 1) and n > 1:
                 q3(n - 1)
-            if ok(n - 3):
-                mx2(n - 3)
             if ok(n - 2):
                 r_s(n - 2)
+                if RV == 0:
+                    r_v(n - 2)
+                r_g(n - 2)
+            if ok(n - 3):
+                q4(n - 3)
+            if ok(n - 2) and RV == 1:
+                r_v(n - 2)
+            if ok(n - 3):
+                mx2(n - 3)
             if ok(n - 3):
                 m_ev(n - 3)
             for t in range(4):
@@ -325,14 +331,13 @@ def tile_additivecoupling_pa_t_kernel(tc, x, h3, W4, b4, W5, b5, out):
                     h_ev(n - 1, t)
             if n == 1:
                 prep5a()
-            if ok(n - 2):
-                r_v(n - 2)
-                r_g(n - 2)
             if ok(n) and n > 0:
                 t_ev(n, True)
                 t_ev(n, False)
             if ok(n - LF):
                 fin(n - LF)
+            if ok(n - 2) and RV == 2:
+                r_v(n - 2)
             if n == 1:
                 prep5b()
             if ok(n + 1):

@@ -16,12 +16,17 @@ IDENT = mybir.ActivationFunctionType.Identity
 
 P = 128
 B, HALF, MID = 8192, 128, 512
-UNITS = [2] + [4] * 15 + [1, 1]
+UNITS = [2] + [4] * 14 + [2, 2, 1, 1]
 NU = len(UNITS)
 G_SHARE = 20
 S_SHARE = 8
 EDGE = 2
-RV = 1
+TL = 0
+L2 = 3
+L3 = 4
+L4 = 4
+L5 = 5
+MPOS = 0
 HEAD = 0
 TAIL_S = 0.5
 W4_V = 352
@@ -63,7 +68,7 @@ def tile_additivecoupling_pa_t_kernel(tc, x, h3, W4, b4, W5, b5, out):
     with ExitStack() as ctx:
         const = ctx.enter_context(tc.tile_pool(name="const", bufs=1))
         inp = ctx.enter_context(tc.tile_pool(name="inp", bufs=8))
-        work = ctx.enter_context(tc.tile_pool(name="work", bufs=3))
+        work = ctx.enter_context(tc.tile_pool(name="work", bufs=4))
         outp = ctx.enter_context(tc.tile_pool(name="outp", bufs=4))
         ps_t = ctx.enter_context(tc.psum_pool(name="ps_t", bufs=2))
         ps_h = ctx.enter_context(tc.psum_pool(name="ps_h", bufs=3))
@@ -298,47 +303,41 @@ def tile_additivecoupling_pa_t_kernel(tc, x, h3, W4, b4, W5, b5, out):
         def ok(u):
             return 0 <= u < NU
 
-        LF = 4
-        for n in range(-5, NU + 6):
-            if ok(n + 5) and n + 5 > 1:
-                load_h(n + 5)
+        for n in range(-7, NU + 9):
+            if ok(n + 6) and n + 6 > 1:
+                load_h(n + 6)
             if ok(n + 1):
                 load_x(n + 1)
-            if n == 0:
+            if n == -TL:
                 t_ev(0, True)
                 t_ev(0, False)
                 prep()
-            if ok(n - LF):
-                m_tr(n - LF)
+            if ok(n - L5):
+                m_tr(n - L5)
             if ok(n - 1) and n > 1:
                 q3(n - 1)
-            if ok(n - 2):
-                r_s(n - 2)
-                if RV == 0:
-                    r_v(n - 2)
-                r_g(n - 2)
-            if ok(n - 3):
-                q4(n - 3)
-            if ok(n - 2) and RV == 1:
-                r_v(n - 2)
-            if ok(n - 3):
-                mx2(n - 3)
-            if ok(n - 3):
-                m_ev(n - 3)
+            if ok(n - L2):
+                r_s(n - L2)
+                r_v(n - L2)
+                r_g(n - L2)
+            if ok(n - L3):
+                q4(n - L3)
+            if ok(n - L4):
+                mx2(n - L4)
             for t in range(4):
                 if ok(n - 1):
                     mx1(n - 1, t)
                     h_ev(n - 1, t)
+                if t == MPOS and ok(n - L4):
+                    m_ev(n - L4)
             if n == 1:
                 prep5a()
-            if ok(n) and n > 0:
-                t_ev(n, True)
-                t_ev(n, False)
-            if ok(n - LF):
-                fin(n - LF)
-            if ok(n - 2) and RV == 2:
-                r_v(n - 2)
+            if ok(n + TL) and n + TL > 0:
+                t_ev(n + TL, True)
+                t_ev(n + TL, False)
+            if ok(n - L5):
+                fin(n - L5)
             if n == 1:
                 prep5b()
-            if ok(n + 1):
-                t_tr(n + 1)
+            if ok(n + TL + 1):
+                t_tr(n + TL + 1)

@@ -18,8 +18,8 @@ P = 128
 B, HALF, MID = 8192, 128, 512
 UNITS = [2] + [4] * 14 + [2, 2, 1, 1]
 NU = len(UNITS)
-G_SHARE = 20
-S_SHARE = 8
+G_SHARE = 23
+S_SHARE = 9
 EDGE = 2
 TL = 0
 L2 = 3
@@ -28,8 +28,11 @@ L4 = 4
 L5 = 5
 MPOS = 0
 HEAD = 0
+VH = 0
 TAIL_S = 0.5
 W4_V = 352
+WSPLIT = 2
+P5 = 2
 
 FLOPS = 2 * B * MID * (MID + HALF)
 
@@ -43,11 +46,13 @@ def g_cols(u):
 
 
 def s_cols(u):
+    if u < VH:
+        return 0
     return 16 * round(UNITS[u] * P * TAIL_S / 16) if u >= NU - EDGE else (0 if edge(u) else 4 * S_SHARE * UNITS[u])
 
 
 def t_on_vector(u, g):
-    return True
+    return u != 1 or g == 1
 
 
 def h_on_vector(u, t):
@@ -124,14 +129,25 @@ def tile_additivecoupling_pa_t_kernel(tc, x, h3, W4, b4, W5, b5, out):
         w5s = const.tile([P, HALF], U8, align_bytes=64)
         bcol = const.tile([P, 8], F32)
 
-        def prep():
-            h = W4_V
-            regroup(nc.vector.tensor_copy, w4g[:, :h, :], w4raw[:, :, :h])
-            regroup(nc.scalar.copy, w4g[:, h:, :], w4raw[:, :, h:])
-            q3(0)
+        def qw(a):
+            b = a + MID // 2
             nc.vector.quantize_mx(
-                out=w4c[:].bitcast(FP8X4), scales=w4s[:], in_=w4g[:].rearrange("p c t -> p (c t)")
+                out=w4c[:, a:b].bitcast(FP8X4),
+                scales=w4s[:, a:b],
+                in_=w4g[:, a:b, :].rearrange("p c t -> p (c t)"),
             )
+
+        def prep():
+            for a in range(0, MID, MID // WSPLIT):
+                m = a + W4_V // WSPLIT
+                b = a + MID // WSPLIT
+                regroup(nc.vector.tensor_copy, w4g[:, a:m, :], w4raw[:, :, a:m])
+                regroup(nc.scalar.copy, w4g[:, m:b, :], w4raw[:, :, m:b])
+                if a == 0:
+                    q3(0)
+                if a > 0:
+                    qw(0)
+            qw(MID // 2)
             bt = ps_m.tile([P, P], BF16, name="bt", tag="mb")
             nc.tensor.transpose(bt[:], bz[:, 0:P], ident_b[:])
             for k in range(2):
@@ -324,20 +340,21 @@ def tile_additivecoupling_pa_t_kernel(tc, x, h3, W4, b4, W5, b5, out):
                 q4(n - L3)
             if ok(n - L4):
                 mx2(n - L4)
+            if ok(n + TL) and n + TL > 0:
+                t_ev(n + TL, False)
             for t in range(4):
                 if ok(n - 1):
                     mx1(n - 1, t)
                     h_ev(n - 1, t)
                 if t == MPOS and ok(n - L4):
                     m_ev(n - L4)
-            if n == 1:
+            if n == P5:
                 prep5a()
             if ok(n + TL) and n + TL > 0:
                 t_ev(n + TL, True)
-                t_ev(n + TL, False)
             if ok(n - L5):
                 fin(n - L5)
-            if n == 1:
+            if n == P5:
                 prep5b()
             if ok(n + TL + 1):
                 t_tr(n + TL + 1)

@@ -33,6 +33,8 @@ TAIL_S = 0.5
 W4_V = 352
 WSPLIT = 2
 P5 = 2
+WARM1 = 3
+WARM2 = 5
 
 FLOPS = 2 * B * MID * (MID + HALF)
 
@@ -101,18 +103,18 @@ def tile_additivecoupling_pa_t_kernel(tc, x, h3, W4, b4, W5, b5, out):
             )
             live["xt", u] = xt
 
-        bz = const.tile([P, 2 * P], BF16)
-        nc.vector.memset(bz[:], 0.0)
         zr = const.tile([P, 2 * P], BF16)
         nc.vector.memset(zr[:], 0.0)
+        bz = const.tile([P, P], BF16)
+        nc.vector.memset(bz[:], 0.0)
         w4raw = const.tile([P, 4, MID], BF16)
         load_h(0)
-        nc.sync.dma_start(out=bz[0:4, 0:P], in_=b4.rearrange("(t p) -> t p", p=P))
-        nc.sync.dma_start(out=bz[4:5, 0:P], in_=b5.unsqueeze(0))
         nc.sync.dma_start(
             out=w4raw[:].rearrange("p (u e) n -> p u e n", u=2),
             in_=W4.rearrange("(u p e) n -> p u e n", u=2, e=2),
         )
+        nc.sync.dma_start(out=bz[0:4, :], in_=b4.rearrange("(t p) -> t p", p=P))
+        nc.sync.dma_start(out=bz[4:5, :], in_=b5.unsqueeze(0))
         w5raw = const.tile([P, 4, HALF], BF16)
         load_h(1)
         nc.sync.dma_start(out=w5raw[:], in_=W5.rearrange("(t p) n -> p t n", p=P))
@@ -128,6 +130,14 @@ def tile_additivecoupling_pa_t_kernel(tc, x, h3, W4, b4, W5, b5, out):
         w5c = const.tile([P, HALF], U32, align_bytes=64)
         w5s = const.tile([P, HALF], U8, align_bytes=64)
         bcol = const.tile([P, 8], F32)
+
+        def zero_zz(n):
+            for k in range(2 * n):
+                nc.tensor.matmul(
+                    zz[k % 2][:, 1, :], lhsT=zr[:, 0:P], rhs=zr[:], start=True, stop=True
+                )
+
+        zero_zz(WARM1)
 
         def qw(a):
             b = a + MID // 2
@@ -149,11 +159,8 @@ def tile_additivecoupling_pa_t_kernel(tc, x, h3, W4, b4, W5, b5, out):
                     qw(0)
             qw(MID // 2)
             bt = ps_m.tile([P, P], BF16, name="bt", tag="mb")
-            nc.tensor.transpose(bt[:], bz[:, 0:P], ident_b[:])
-            for k in range(2):
-                nc.tensor.matmul(
-                    zz[k][:, 1, :], lhsT=zr[:, 0:P], rhs=zr[:], start=True, stop=True
-                )
+            nc.tensor.transpose(bt[:], bz[:], ident_b[:])
+            zero_zz(WARM2)
             nc.vector.tensor_copy(out=bcol[:], in_=bt[:, 0:8])
 
         def prep5a():
@@ -252,8 +259,8 @@ def tile_additivecoupling_pa_t_kernel(tc, x, h3, W4, b4, W5, b5, out):
                 tok = work.tile([P, 1], F32, name="tok", tag="tok")
                 nc.vector.memset(tok[:], 1.0)
                 nc.gpsimd.tensor_scalar(
-                    out=live["g4", u][:, w - n : w, :],
-                    in0=live["h4p", u][:, :, w - n : w].rearrange("p t c -> p c t"),
+                    out=live["g4", u][:, w - n : w, :].rearrange("p (c i) t -> p c t i", i=4),
+                    in0=live["h4p", u][:, :, w - n : w].rearrange("p t (c i) -> p c t i", i=4),
                     scalar1=tok[:], scalar2=0.0, op0=MULT, op1=ADD,
                 )
 

@@ -18,8 +18,8 @@ P = 128
 B, HALF, MID = 8192, 128, 512
 UNITS = [2] + [4] * 14 + [2, 2, 1, 1]
 NU = len(UNITS)
-G_SHARE = 23
-S_SHARE = 9
+G_SHARE = 25
+S_SHARE = 7
 EDGE = 2
 TL = 0
 L2 = 3
@@ -76,6 +76,7 @@ def tile_additivecoupling_pa_t_kernel(tc, x, h3, W4, b4, W5, b5, out):
         const = ctx.enter_context(tc.tile_pool(name="const", bufs=1))
         inp = ctx.enter_context(tc.tile_pool(name="inp", bufs=8))
         work = ctx.enter_context(tc.tile_pool(name="work", bufs=4))
+        g4p = ctx.enter_context(tc.tile_pool(name="g4p", bufs=1))
         outp = ctx.enter_context(tc.tile_pool(name="outp", bufs=4))
         ps_t = ctx.enter_context(tc.psum_pool(name="ps_t", bufs=2))
         ps_h = ctx.enter_context(tc.psum_pool(name="ps_h", bufs=3))
@@ -240,7 +241,7 @@ def tile_additivecoupling_pa_t_kernel(tc, x, h3, W4, b4, W5, b5, out):
                 )
 
         def r_s(u):
-            live["g4", u] = work.tile([P, 4 * P, 4], BF16, name="g4", tag="g4", align_bytes=64)
+            live["g4", u] = g4p.tile([P, 4 * P, 4], BF16, name="g4", tag="g4", align_bytes=64)
             ws = s_cols(u)
             if ws > 0:
                 regroup(nc.scalar.copy, live["g4", u][:, :ws, :], live["h4p", u][:, :, :ws])
@@ -256,12 +257,10 @@ def tile_additivecoupling_pa_t_kernel(tc, x, h3, W4, b4, W5, b5, out):
             w = UNITS[u] * P
             n = g_cols(u)
             if n > 0:
-                tok = work.tile([P, 1], F32, name="tok", tag="tok")
-                nc.vector.memset(tok[:], 1.0)
                 nc.gpsimd.tensor_scalar(
                     out=live["g4", u][:, w - n : w, :].rearrange("p (c i) t -> p c t i", i=4),
                     in0=live["h4p", u][:, :, w - n : w].rearrange("p t (c i) -> p c t i", i=4),
-                    scalar1=tok[:], scalar2=0.0, op0=MULT, op1=ADD,
+                    scalar1=1.0, scalar2=0.0, op0=MULT, op1=ADD,
                 )
 
         def q4(u):
@@ -337,14 +336,14 @@ def tile_additivecoupling_pa_t_kernel(tc, x, h3, W4, b4, W5, b5, out):
                 prep()
             if ok(n - L5):
                 m_tr(n - L5)
+            if ok(n - L3):
+                q4(n - L3)
             if ok(n - 1) and n > 1:
                 q3(n - 1)
             if ok(n - L2):
                 r_s(n - L2)
                 r_v(n - L2)
                 r_g(n - L2)
-            if ok(n - L3):
-                q4(n - L3)
             if ok(n - L4):
                 mx2(n - L4)
             if ok(n + TL) and n + TL > 0:

@@ -34,7 +34,7 @@ W4_V = 352
 WSPLIT = 2
 P5 = 2
 WARM1 = 3
-WARM2 = 5
+WARM2 = 2
 
 FLOPS = 2 * B * MID * (MID + HALF)
 
@@ -335,6 +335,7 @@ def tile_additivecoupling_pa_t_kernel(tc, x, h3, W4, b4, W5, b5, out):
                 t_ev(0, False)
                 prep()
             if ok(n - L5):
+                zero_zz(1)
                 m_tr(n - L5)
             if ok(n - L3):
                 q4(n - L3)

from contextlib import ExitStack

import concourse.mybir as mybir
from concourse.masks import make_identity

FP8X4 = mybir.dt.float8_e4m3fn_x4
BF16 = mybir.dt.bfloat16
F32 = mybir.dt.float32
U32 = mybir.dt.uint32
U8 = mybir.dt.uint8
ADD = mybir.AluOpType.add
MULT = mybir.AluOpType.mult
MAX = mybir.AluOpType.max
RELU = mybir.ActivationFunctionType.Relu
IDENT = mybir.ActivationFunctionType.Identity

P = 128
B, HALF, MID = 8192, 128, 512
UNITS = [2] + [4] * 14 + [2, 2, 1, 1]
NU = len(UNITS)
G_SHARE = 25
S_SHARE = 7
EDGE = 2
TL = 0
L2 = 3
L3 = 4
L4 = 4
L5 = 5
MPOS = 0
HEAD = 0
VH = 0
TAIL_S = 0.5
W4_V = 352
WSPLIT = 2
P5 = 2
WARM1 = 3
WARM2 = 2

FLOPS = 2 * B * MID * (MID + HALF)


def edge(u):
    return u < HEAD or u >= NU - EDGE


def g_cols(u):
    return 0 if edge(u) else 4 * G_SHARE * UNITS[u]


def s_cols(u):
    if u < VH:
        return 0
    return 16 * round(UNITS[u] * P * TAIL_S / 16) if u >= NU - EDGE else (0 if edge(u) else 4 * S_SHARE * UNITS[u])


def t_on_vector(u, g):
    return u != 1 or g == 1


def h_on_vector(u, t):
    return False


def regroup(eng_copy, dst, src):
    eng_copy(
        out=dst.rearrange("p (c i) t -> p c t i", i=4),
        in_=src.rearrange("p t (c i) -> p c t i", i=4),
    )


def tile_additivecoupling_pa_t_kernel(tc, x, h3, W4, b4, W5, b5, out):
    nc = tc.nc
    assert sum(UNITS) * P == B
    row0 = [P * sum(UNITS[:u]) for u in range(NU)]
    with ExitStack() as ctx:
        const = ctx.enter_context(tc.tile_pool(name="const", bufs=1))
        inp = ctx.enter_context(tc.tile_pool(name="inp", bufs=8))
        work = ctx.enter_context(tc.tile_pool(name="work", bufs=4))
        g4p = ctx.enter_context(tc.tile_pool(name="g4p", bufs=1))
        outp = ctx.enter_context(tc.tile_pool(name="outp", bufs=4))
        ps_t = ctx.enter_context(tc.psum_pool(name="ps_t", bufs=2))
        ps_h = ctx.enter_context(tc.psum_pool(name="ps_h", bufs=3))
        ps_m = ctx.enter_context(tc.psum_pool(name="ps_m", bufs=1))
        ps_z = ctx.enter_context(tc.psum_pool(name="ps_z", bufs=1))
        ctx.enter_context(tc.manual_schedule())

        live = {}

        def load_h(u):
            nt = UNITS[u]
            ht = inp.tile([P, 4 * MID], BF16, name="ht", tag="ht")
            nc.sync.dma_start(
                out=ht[:, : nt * MID],
                in_=h3[row0[u] : row0[u] + nt * P, :].rearrange("(p i) k -> p (i k)", i=nt),
            )
            live["ht", u] = ht

        def load_x(u):
            nt = UNITS[u]
            xt = inp.tile([P, 4 * 2 * HALF], BF16, name="xt", tag="xt")
            nc.sync.dma_start(
                out=xt[:, : nt * 2 * HALF],
                in_=x[row0[u] : row0[u] + nt * P, :].rearrange("(p i) c -> p (i c)", i=nt),
            )
            live["xt", u] = xt

        zr = const.tile([P, 2 * P], BF16)
        nc.vector.memset(zr[:], 0.0)
        bz = const.tile([P, P], BF16)
        nc.vector.memset(bz[:], 0.0)
        w4raw = const.tile([P, 4, MID], BF16)
        load_h(0)
        nc.sync.dma_start(
            out=w4raw[:].rearrange("p (u e) n -> p u e n", u=2),
            in_=W4.rearrange("(u p e) n -> p u e n", u=2, e=2),
        )
        nc.sync.dma_start(out=bz[0:4, :], in_=b4.rearrange("(t p) -> t p", p=P))
        nc.sync.dma_start(out=bz[4:5, :], in_=b5.unsqueeze(0))
        w5raw = const.tile([P, 4, HALF], BF16)
        load_h(1)
        nc.sync.dma_start(out=w5raw[:], in_=W5.rearrange("(t p) n -> p t n", p=P))
        ident_f = const.tile([P, P], F32)
        make_identity(nc, ident_f[:])
        ident_b = const.tile([P, P], BF16)
        make_identity(nc, ident_b[:])
        zz = [ps_z.tile([P, 2, 2 * P], F32, name="zz%d" % k) for k in range(2)]
        w4g = const.tile([P, MID, 4], BF16, align_bytes=64)
        w4c = const.tile([P, MID], U32, align_bytes=64)
        w4s = const.tile([P, MID], U8, align_bytes=64)
        w5g = const.tile([P, HALF, 4], BF16, align_bytes=64)
        w5c = const.tile([P, HALF], U32, align_bytes=64)
        w5s = const.tile([P, HALF], U8, align_bytes=64)
        bcol = const.tile([P, 8], F32)

        def zero_zz(n):
            for k in range(2 * n):
                nc.tensor.matmul(
                    zz[k % 2][:, 1, :], lhsT=zr[:, 0:P], rhs=zr[:], start=True, stop=True
                )

        zero_zz(WARM1)

        def qw(a):
            b = a + MID // 2
            nc.vector.quantize_mx(
                out=w4c[:, a:b].bitcast(FP8X4),
                scales=w4s[:, a:b],
                in_=w4g[:, a:b, :].rearrange("p c t -> p (c t)"),
            )

        def prep():
            for a in range(0, MID, MID // WSPLIT):
                m = a + W4_V // WSPLIT
                b = a + MID // WSPLIT
                regroup(nc.vector.tensor_copy, w4g[:, a:m, :], w4raw[:, :, a:m])
                regroup(nc.scalar.copy, w4g[:, m:b, :], w4raw[:, :, m:b])
                if a == 0:
                    q3(0)
                if a > 0:
                    qw(0)
            qw(MID // 2)
            bt = ps_m.tile([P, P], BF16, name="bt", tag="mb")
            nc.tensor.transpose(bt[:], bz[:], ident_b[:])
            zero_zz(WARM2)
            nc.vector.tensor_copy(out=bcol[:], in_=bt[:, 0:8])

        def prep5a():
            regroup(nc.vector.tensor_copy, w5g[:], w5raw[:])

        def prep5b():
            nc.vector.quantize_mx(
                out=w5c[:].bitcast(FP8X4), scales=w5s[:], in_=w5g[:].rearrange("p c t -> p (c t)")
            )

        def groups(u):
            return [(i0, min(2, UNITS[u] - i0)) for i0 in range(0, UNITS[u], 2)]

        def t_tr(u):
            hw = live["ht", u][:].bitcast(F32)
            for g, (i0, n2) in enumerate(groups(u)):
                tp = ps_t.tile([P, 2, 2 * P], F32, name="tp", tag="tp")
                for ii in range(n2):
                    for u2 in range(2):
                        c0 = 256 * (i0 + ii) + P * u2
                        nc.tensor.transpose(
                            tp[:, u2, ii * P : (ii + 1) * P], hw[:, c0 : c0 + P], ident_f[:]
                        )
                live["tp", u, g] = tp

        def t_ev(u, vec):
            if ("g3", u) not in live:
                live["g3", u] = work.tile([P, 16 * P], BF16, name="g3", tag="g3", align_bytes=64)
            g3w = live["g3", u][:].bitcast(F32)
            for g, (i0, n2) in enumerate(groups(u)):
                if t_on_vector(u, g) != vec:
                    continue
                cp = nc.vector.tensor_copy if vec else nc.scalar.copy
                cp(
                    out=g3w[:, 256 * i0 : 256 * (i0 + n2)].rearrange("p (r u) -> p r u", u=2),
                    in_=live["tp", u, g][:, :, : n2 * P].rearrange("p u r -> p r u"),
                )

        def q3(u):
            w = UNITS[u] * P
            c3 = work.tile([P, 4 * P], U32, name="c3", tag="c3", align_bytes=64)
            s3 = work.tile([P, 4 * P], U8, name="s3", tag="s3", align_bytes=64)
            nc.vector.quantize_mx(
                out=c3[:, :w].bitcast(FP8X4), scales=s3[:, :w], in_=live["g3", u][:, : 4 * w]
            )
            live["c3", u] = c3
            live["s3", u] = s3

        def mx1(u, t):
            w = UNITS[u] * P
            hb = ps_h.tile([P, 4 * P], F32, name="hb", tag="hb")
            nc.tensor.matmul_mx(
                out=hb[:, :w],
                lhsT=w4c[:, t * P : (t + 1) * P].bitcast(FP8X4),
                lhsT_scale=w4s[:, t * P : (t + 1) * P],
                rhs=live["c3", u][:, :w].bitcast(FP8X4),
                rhs_scale=live["s3", u][:, :w],
                start=True,
                stop=True,
            )
            live["hb", u, t] = hb

        def h_ev(u, t):
            w = UNITS[u] * P
            if t == 0:
                live["h4p", u] = work.tile([P, 4, 4 * P], BF16, name="h4p", tag="h4p")
            h4p = live["h4p", u]
            hb = live["hb", u, t]
            if h_on_vector(u, t):
                nc.vector.tensor_scalar(
                    out=h4p[:, t, :w], in0=hb[:, :w], scalar1=bcol[:, t : t + 1], scalar2=0.0,
                    op0=ADD, op1=MAX,
                )
            else:
                nc.scalar.activation(
                    out=h4p[:, t, :w], in_=hb[:, :w], func=RELU, bias=bcol[:, t : t + 1], scale=1.0
                )

        def r_s(u):
            live["g4", u] = g4p.tile([P, 4 * P, 4], BF16, name="g4", tag="g4", align_bytes=64)
            ws = s_cols(u)
            if ws > 0:
                regroup(nc.scalar.copy, live["g4", u][:, :ws, :], live["h4p", u][:, :, :ws])

        def r_v(u):
            w = UNITS[u] * P
            a = s_cols(u)
            b = w - g_cols(u)
            if a < b:
                regroup(nc.vector.tensor_copy, live["g4", u][:, a:b, :], live["h4p", u][:, :, a:b])

        def r_g(u):
            w = UNITS[u] * P
            n = g_cols(u)
            if n > 0:
                nc.gpsimd.tensor_scalar(
                    out=live["g4", u][:, w - n : w, :].rearrange("p (c i) t -> p c t i", i=4),
                    in0=live["h4p", u][:, :, w - n : w].rearrange("p t (c i) -> p c t i", i=4),
                    scalar1=1.0, scalar2=0.0, op0=MULT, op1=ADD,
                )

        def q4(u):
            w = UNITS[u] * P
            c4 = work.tile([P, 4 * P], U32, name="c4", tag="c4", align_bytes=64)
            s4 = work.tile([P, 4 * P], U8, name="s4", tag="s4", align_bytes=64)
            nc.vector.quantize_mx(
                out=c4[:, :w].bitcast(FP8X4),
                scales=s4[:, :w],
                in_=live["g4", u][:, :w, :].rearrange("p c t -> p (c t)"),
            )
            live["c4", u] = c4
            live["s4", u] = s4

        def mx2(u):
            w = UNITS[u] * P
            mb = ps_m.tile([P, 4 * P], F32, name="mb", tag="mb")
            nc.tensor.matmul_mx(
                out=mb[:, :w],
                lhsT=w5c[:].bitcast(FP8X4),
                lhsT_scale=w5s[:],
                rhs=live["c4", u][:, :w].bitcast(FP8X4),
                rhs_scale=live["s4", u][:, :w],
                start=True,
                stop=True,
            )
            live["mb", u] = mb

        def m_ev(u):
            w = UNITS[u] * P
            mt = work.tile([P, 4 * P], F32, name="mt", tag="mt")
            nc.scalar.activation(
                out=mt[:, :w], in_=live["mb", u][:, :w], func=IDENT, bias=bcol[:, 4:5], scale=1.0
            )
            live["mt", u] = mt

        def m_tr(u):
            for g, (i0, n2) in enumerate(groups(u)):
                for ii in range(n2):
                    nc.tensor.transpose(
                        zz[g][:, 0, ii * P : (ii + 1) * P],
                        live["mt", u][:, (i0 + ii) * P : (i0 + ii + 1) * P],
                        ident_f[:],
                    )

        def fin(u):
            nt = UNITS[u]
            ot = outp.tile([P, 4 * 2 * HALF], F32, name="ot", tag="ot")
            for g, (i0, n2) in enumerate(groups(u)):
                a, b = 2 * P * i0, 2 * P * (i0 + n2)
                nc.vector.tensor_tensor(
                    out=ot[:, a:b].rearrange("p (q e) -> p q e", e=2),
                    in0=zz[g][:, :, : n2 * P].rearrange("p e q -> p q e"),
                    in1=live["xt", u][:, a:b].rearrange("p (q e) -> p q e", e=2),
                    op=ADD,
                )
            nc.sync.dma_start(
                out=out[row0[u] : row0[u] + nt * P, :].rearrange("(p i) c -> p (i c)", i=nt),
                in_=ot[:, : nt * 2 * HALF],
            )

        def ok(u):
            return 0 <= u < NU

        for n in range(-7, NU + 9):
            if ok(n + 6) and n + 6 > 1:
                load_h(n + 6)
            if ok(n + 1):
                load_x(n + 1)
            if n == -TL:
                t_ev(0, True)
                t_ev(0, False)
                prep()
            if ok(n - L5):
                zero_zz(1)
                m_tr(n - L5)
            if ok(n - L3):
                q4(n - L3)
            if ok(n - 1) and n > 1:
                q3(n - 1)
            if ok(n - L2):
                r_s(n - L2)
                r_v(n - L2)
                r_g(n - L2)
            if ok(n - L4):
                mx2(n - L4)
            if ok(n + TL) and n + TL > 0:
                t_ev(n + TL, False)
            for t in range(4):
                if ok(n - 1):
                    mx1(n - 1, t)
                    h_ev(n - 1, t)
                if t == MPOS and ok(n - L4):
                    m_ev(n - L4)
            if n == P5:
                prep5a()
            if ok(n + TL) and n + TL > 0:
                t_ev(n + TL, True)
            if ok(n - L5):
                fin(n - L5)
            if n == P5:
                prep5b()
            if ok(n + TL + 1):
                t_tr(n + TL + 1)
